import numpy as np
import ml_dtypes


def mxq(x, axis, fmt="e4m3"):
    dtype, down = {"e4m3": (ml_dtypes.float8_e4m3fn, 7), "e5m2": (ml_dtypes.float8_e5m2, 14)}[fmt]
    v = np.moveaxis(np.asarray(x, np.float32).astype(ml_dtypes.bfloat16).astype(np.float64), axis, -1)
    blocks = v.reshape(v.shape[:-1] + (-1, 32))
    amax = np.abs(blocks).max(-1, keepdims=True)
    byte = np.maximum(np.where(amax > 0, np.frexp(amax)[1] - 1 + 127, 0) - down, 1)
    scale = np.exp2(byte - 127.0)
    codes = (blocks / scale).astype(np.float32).astype(dtype).astype(np.float64)
    return np.moveaxis((codes * scale).reshape(v.shape), -1, axis)


WIDE = False


def mx_kscale(k):
    if not WIDE:
        return np.ones(k)
    levels = np.array([10, -10, 5, -5, 0])
    if k % 512:
        return np.exp2(np.random.permutation(np.resize(levels, k // 32))).repeat(32)
    a = np.empty((k // 512, 16))
    for p in range(k // 512):
        a[p, :8] = np.random.permutation(np.resize(levels, 8))
        for g in range(8):
            far = levels[np.abs(levels - a[p, g]) >= 10]
            a[p, g + 8] = far[np.random.randint(len(far))]
    return np.exp2(a.ravel()).repeat(32)


BF16 = ml_dtypes.bfloat16


def bf(x):
    return np.asarray(x, np.float32).astype(BF16)


def f64(x):
    return np.asarray(x).astype(np.float64)


B, S, H, O, W = 8, 2048, 512, 128, 8


def setup_inputs():
    s = mx_kscale(H)
    return {"hidden_states": bf(np.random.standard_normal((B, S, H)) * s),
            "gate_proj": bf(np.random.standard_normal((O, H)) / np.sqrt(H) / s[None, :]),
            "world_size": W}


def core(hidden_states, gate_proj, world_size):
    h = gate_proj.shape[1]
    view = f64(hidden_states).reshape(-1, h)
    mm = mxq(view, 1, "e4m3") @ mxq(f64(gate_proj), 1, "e4m3").T
    n, o = mm.shape
    out = mm.reshape(world_size, n // world_size, o).sum(axis=0)
    return out


def e4m3fn_bytes(y):
    return np.clip(np.asarray(y, np.float64), -448.0, 448.0).astype(np.float32).astype(ml_dtypes.float8_e4m3fn).view(np.uint8)


def reference(hidden_states, gate_proj, world_size):
    out = core(hidden_states, gate_proj, world_size)
    s = np.max(np.abs(out)) / 448.0
    return out, e4m3fn_bytes(out / s)

@@ -1,0 +1,224 @@
+from contextlib import ExitStack
+
+import concourse.masks as masks
+import concourse.mybir as mybir
+
+F32 = mybir.dt.float32
+BF16 = mybir.dt.bfloat16
+U32 = mybir.dt.uint32
+U8 = mybir.dt.uint8
+FP8X4 = mybir.dt.float8_e4m3fn_x4
+FP8 = mybir.dt.float8_e4m3fn
+ALU = mybir.AluOpType
+ACT = mybir.ActivationFunctionType
+AX = mybir.AxisListType
+
+P = 128
+R = 8
+S = 2048
+H = 512
+O = 128
+I = S // P
+NL = 4
+NB = I // NL
+W = H // 2
+
+FLOPS = 2 * R * S * H * O
+
+V_CAST = 1344
+
+
+def tile_testmmrsmodel_t_kernel(tc, hidden_states, gate_proj, world_size, out_0, out_1):
+    nc = tc.nc
+    assert world_size == R
+
+    hs = hidden_states.rearrange("r (p i) k -> p r (i k)", i=I)
+    o0 = out_0.rearrange("(p i) o -> p (i o)", i=I)
+    o1 = out_1.rearrange("(p i) o -> p (i o)", i=I)
+
+    pieces = []
+    for ib in range(NB):
+        for r0 in range(0, R, 2):
+            if ib == 0 and r0 == 0:
+                pieces.extend([(ib, 0, 1, 0, 2), (ib, 0, 1, 2, 2), (ib, 1, 1, 0, 4)])
+            elif ib == NB - 1 and r0 == R - 2:
+                pieces.extend([(ib, r0, 1, 0, 4), (ib, r0 + 1, 1, 0, 2), (ib, r0 + 1, 1, 2, 2)])
+            else:
+                pieces.append((ib, r0, 2, 0, 4))
+    n = len(pieces)
+    nre = []
+    for q in range(n):
+        nu = pieces[q][2] * pieces[q][4]
+        nre.append(0 if q in (0, 1, n - 2, n - 1) else nu - nu // 4)
+
+    with ExitStack() as ctx:
+        ctx.enter_context(tc.manual_schedule())
+        const = ctx.enter_context(tc.tile_pool(name="const", bufs=1))
+        rawp = ctx.enter_context(tc.tile_pool(name="rawp", bufs=1))
+        work = ctx.enter_context(tc.tile_pool(name="work", bufs=3))
+        tpp = ctx.enter_context(tc.psum_pool(name="tpp", bufs=4))
+        accp = ctx.enter_context(tc.psum_pool(name="accp", bufs=1))
+
+        ident = const.tile([P, P], F32, name="ident")
+        masks.make_identity(nc, ident[:])
+        zero = const.tile([P, 1], F32, name="zero")
+        nc.vector.memset(zero[:], 0.0)
+
+        g_raw = const.tile([P, H], BF16, name="g_raw")
+        nc.sync.dma_start(out=g_raw[:], in_=gate_proj)
+        raw = []
+        for q in range(n):
+            ib, r0, nr, l0, nl = pieces[q]
+            t = rawp.tile([P, nr * nl * H], BF16, name="raw%d" % q)
+            i0 = ib * NL + l0
+            nc.sync.dma_start(
+                out=t[:].rearrange("p (a x) -> p a x", a=nr),
+                in_=hs[:, r0:r0 + nr, i0 * H:(i0 + nl) * H],
+            )
+            raw.append(t)
+
+        g_words = g_raw[:].bitcast(F32)
+        g_tp = tpp.tile([P, 2, 2, P], F32, name="tp", tag="tp")
+        for u in range(2):
+            nc.tensor.transpose(g_tp[:, 0, u, :], g_words[:, u:W:2], ident[:])
+        g_gq = const.tile([P, 4 * O], BF16, name="g_gq", align_bytes=64)
+        nc.scalar.copy(
+            out=g_gq[:].bitcast(F32).rearrange("p (r u) -> p r u", u=2),
+            in_=g_tp[:, 0, :, :].rearrange("p u r -> p r u"),
+        )
+        g_codes = const.tile([P, O], U32, name="g_codes", align_bytes=64)
+        g_scales = const.tile([P, O], U8, name="g_scales", align_bytes=64)
+        nc.vector.quantize_mx(out=g_codes[:].bitcast(FP8X4), scales=g_scales[:], in_=g_gq[:])
+
+        acc = []
+        for l in range(NL):
+            a = accp.tile([P, NB, O], F32, name="acc%d" % l)
+            acc.append(a)
+        out_sb = const.tile([P, I * O], F32, name="out_sb")
+        pm = const.tile([P, NB], F32, name="pm")
+
+        xr = [None] * n
+        tps = [None] * n
+        gqs = [None] * n
+        cds = [None] * n
+        scs = [None] * n
+
+        def units(q):
+            ib, r0, nr, l0, nl = pieces[q]
+            return [(ib, l0 + b, r0 + a) for a in range(nr) for b in range(nl)]
+
+        def reorder(q):
+            nu = len(units(q))
+            if nre[q] == 0:
+                return
+            t = work.tile([P, nre[q], 2, P], F32, name="xr", tag="xr")
+            nc.vector.tensor_copy(
+                out=t[:],
+                in_=raw[q][:].bitcast(F32).rearrange("p (v w u) -> p v u w", v=nu, u=2)[:, 0:nre[q], :, :],
+            )
+            xr[q] = t
+
+        def transpose(q):
+            nu = len(units(q))
+            words = raw[q][:].bitcast(F32)
+            banks = []
+            for j in range(nu // 2):
+                b = tpp.tile([P, 2, 2, P], F32, name="tp", tag="tp")
+                for a in range(2):
+                    v = 2 * j + a
+                    for u in range(2):
+                        if v >= nre[q]:
+                            src = words[:, v * W + u:(v + 1) * W:2]
+                        else:
+                            src = xr[q][:, v, u, :]
+                        nc.tensor.transpose(b[:, a, u, :], src, ident[:])
+                banks.append(b)
+            tps[q] = banks
+
+        def evacuate(q):
+            nu = len(units(q))
+            g = work.tile([P, nu * 4 * P], BF16, name="gq", tag="gq", align_bytes=64)
+            gw = g[:].bitcast(F32).rearrange("p (v r u) -> p v r u", v=nu, u=2)
+            for j in range(nu // 2):
+                nc.scalar.copy(
+                    out=gw[:, 2 * j:2 * j + 2, :, :],
+                    in_=tps[q][j][:].rearrange("p v u r -> p v r u"),
+                )
+            gqs[q] = g
+
+        def quantize(q):
+            nu = len(units(q))
+            c = work.tile([P, nu * P], U32, name="cd", tag="cd", align_bytes=64)
+            s = work.tile([P, nu * P], U8, name="sc", tag="sc", align_bytes=64)
+            nc.vector.quantize_mx(out=c[:].bitcast(FP8X4), scales=s[:], in_=gqs[q][:])
+            cds[q] = c
+            scs[q] = s
+
+        def multiply(q):
+            closed = []
+            for v, (ib, l, r) in enumerate(units(q)):
+                nc.tensor.matmul_mx(
+                    out=acc[l][:, ib, :],
+                    lhsT=cds[q][:, v * P:(v + 1) * P].bitcast(FP8X4),
+                    lhsT_scale=scs[q][:, v * P:(v + 1) * P],
+                    rhs=g_codes[:].bitcast(FP8X4),
+                    rhs_scale=g_scales[:],
+                    start=(r == 0),
+                    stop=(r == R - 1),
+                )
+                if r == R - 1:
+                    closed.append((ib, l))
+            for ib, l in closed:
+                i = ib * NL + l
+                nc.scalar.copy(out=out_sb[:, i * O:(i + 1) * O], in_=acc[l][:, ib, :])
+            return closed
+
+        def finish_block(ib):
+            cols = slice(ib * NL * O, (ib + 1) * NL * O)
+            nc.vector.tensor_reduce(
+                out=pm[:, ib:ib + 1], in_=out_sb[:, cols], axis=AX.X, op=ALU.max,
+                apply_absolute_value=True,
+            )
+            nc.sync.dma_start(out=o0[:, cols], in_=out_sb[:, cols])
+
+        pending = []
+        for s in range(-1, n + 3):
+            if 0 <= s - 2 < n:
+                quantize(s - 2)
+            for ib in pending:
+                finish_block(ib)
+            pending = []
+            if s + 1 < n:
+                reorder(s + 1)
+            if 0 <= s - 1 < n:
+                transpose(s - 1)
+                evacuate(s - 1)
+            if 0 <= s - 3 < n:
+                closed = multiply(s - 3)
+                if (closed and closed[-1][1] == NL - 1):
+                    pending.append(closed[-1][0])
+        for ib in pending:
+            finish_block(ib)
+
+        pmx = const.tile([P, 1], F32, name="pmx")
+        nc.vector.tensor_reduce(out=pmx[:], in_=pm[:], axis=AX.X, op=ALU.max)
+        bc = tpp.tile([P, P], F32, name="tp", tag="tp")
+        nc.tensor.transpose(bc[:], pmx[:, 0:1].to_broadcast([P, P]), ident[:])
+        junk = const.tile([P, P], F32, name="junk")
+        sc448 = const.tile([P, 1], F32, name="sc448")
+        nc.vector.tensor_scalar(
+            out=junk[:], in0=bc[:], scalar1=1.0 / 448.0, scalar2=None,
+            op0=ALU.mult, op1=ALU.max, accum_out=sc448[:, 0:1],
+        )
+        fac = const.tile([P, 1], F32, name="fac")
+        nc.vector.reciprocal(out=fac[:], in_=sc448[:])
+        o8 = const.tile([P, I * O], FP8, name="o8")
+        nc.vector.tensor_scalar(
+            out=o8[:, 0:V_CAST], in0=out_sb[:, 0:V_CAST], scalar1=fac[:, 0:1], scalar2=None,
+            op0=ALU.mult, saturate=False,
+        )
+        nc.scalar.activation(
+            out=o8[:, V_CAST:], in_=out_sb[:, V_CAST:], func=ACT.Identity,
+            scale=fac[:, 0:1], bias=zero[:, 0:1], saturate=False,
+        )
+        nc.sync.dma_start(out=o1, in_=o8[:].bitcast(U8))

@@ -26,6 +26,7 @@ W = H // 2
 FLOPS = 2 * R * S * H * O
 
 V_CAST = 1344
+NPART = 8
 
 
 def tile_testmmrsmodel_t_kernel(tc, hidden_states, gate_proj, world_size, out_0, out_1):
@@ -42,14 +43,14 @@ def tile_testmmrsmodel_t_kernel(tc, hidden_states, gate_proj, world_size, out_0,
             if ib == 0 and r0 == 0:
                 pieces.extend([(ib, 0, 1, 0, 2), (ib, 0, 1, 2, 2), (ib, 1, 1, 0, 4)])
             elif ib == NB - 1 and r0 == R - 2:
-                pieces.extend([(ib, r0, 1, 0, 4), (ib, r0 + 1, 1, 0, 2), (ib, r0 + 1, 1, 2, 2)])
+                pieces.extend([(ib, r0, 1, 0, 4), (ib, r0 + 1, 1, 0, 2), (ib, r0 + 1, 1, 2, 1), (ib, r0 + 1, 1, 3, 1)])
             else:
                 pieces.append((ib, r0, 2, 0, 4))
     n = len(pieces)
     nre = []
     for q in range(n):
         nu = pieces[q][2] * pieces[q][4]
-        nre.append(0 if q in (0, 1, n - 2, n - 1) else nu - nu // 4)
+        nre.append(0 if (q < 2 or q >= n - 3) else nu - (3 * nu) // 8)
 
     with ExitStack() as ctx:
         ctx.enter_context(tc.manual_schedule())
@@ -65,7 +66,6 @@ def tile_testmmrsmodel_t_kernel(tc, hidden_states, gate_proj, world_size, out_0,
         nc.vector.memset(zero[:], 0.0)
 
         g_raw = const.tile([P, H], BF16, name="g_raw")
-        nc.sync.dma_start(out=g_raw[:], in_=gate_proj)
         raw = []
         for q in range(n):
             ib, r0, nr, l0, nl = pieces[q]
@@ -76,26 +76,30 @@ def tile_testmmrsmodel_t_kernel(tc, hidden_states, gate_proj, world_size, out_0,
                 in_=hs[:, r0:r0 + nr, i0 * H:(i0 + nl) * H],
             )
             raw.append(t)
+            if q == 1:
+                nc.sync.dma_start(out=g_raw[:], in_=gate_proj)
 
-        g_words = g_raw[:].bitcast(F32)
-        g_tp = tpp.tile([P, 2, 2, P], F32, name="tp", tag="tp")
-        for u in range(2):
-            nc.tensor.transpose(g_tp[:, 0, u, :], g_words[:, u:W:2], ident[:])
-        g_gq = const.tile([P, 4 * O], BF16, name="g_gq", align_bytes=64)
-        nc.scalar.copy(
-            out=g_gq[:].bitcast(F32).rearrange("p (r u) -> p r u", u=2),
-            in_=g_tp[:, 0, :, :].rearrange("p u r -> p r u"),
-        )
         g_codes = const.tile([P, O], U32, name="g_codes", align_bytes=64)
         g_scales = const.tile([P, O], U8, name="g_scales", align_bytes=64)
-        nc.vector.quantize_mx(out=g_codes[:].bitcast(FP8X4), scales=g_scales[:], in_=g_gq[:])
+
+        def prepare_gate():
+            g_words = g_raw[:].bitcast(F32)
+            g_tp = tpp.tile([P, 2, 2, P], F32, name="tp", tag="tp")
+            for u in range(2):
+                nc.tensor.transpose(g_tp[:, 0, u, :], g_words[:, u:W:2], ident[:])
+            g_gq = const.tile([P, 4 * O], BF16, name="g_gq", align_bytes=64)
+            nc.scalar.copy(
+                out=g_gq[:].bitcast(F32).rearrange("p (r u) -> p r u", u=2),
+                in_=g_tp[:, 0, :, :].rearrange("p u r -> p r u"),
+            )
+            nc.vector.quantize_mx(out=g_codes[:].bitcast(FP8X4), scales=g_scales[:], in_=g_gq[:])
 
         acc = []
         for l in range(NL):
             a = accp.tile([P, NB, O], F32, name="acc%d" % l)
             acc.append(a)
-        out_sb = const.tile([P, I * O], F32, name="out_sb")
-        pm = const.tile([P, NB], F32, name="pm")
+        out_sb = const.tile([P, I * O + NPART], F32, name="out_sb")
+        pmx = const.tile([P, 1], F32, name="pmx")
 
         xr = [None] * n
         tps = [None] * n
@@ -111,10 +115,10 @@ def tile_testmmrsmodel_t_kernel(tc, hidden_states, gate_proj, world_size, out_0,
             nu = len(units(q))
             if nre[q] == 0:
                 return
-            t = work.tile([P, nre[q], 2, P], F32, name="xr", tag="xr")
+            t = work.tile([P, 2, nre[q], P], F32, name="xr", tag="xr")
             nc.vector.tensor_copy(
                 out=t[:],
-                in_=raw[q][:].bitcast(F32).rearrange("p (v w u) -> p v u w", v=nu, u=2)[:, 0:nre[q], :, :],
+                in_=raw[q][:].bitcast(F32).rearrange("p (v w u) -> p u v w", v=nu, u=2)[:, :, 0:nre[q], :],
             )
             xr[q] = t
 
@@ -122,16 +126,15 @@ def tile_testmmrsmodel_t_kernel(tc, hidden_states, gate_proj, world_size, out_0,
             nu = len(units(q))
             words = raw[q][:].bitcast(F32)
             banks = []
-            for j in range(nu // 2):
+            for v0 in range(0, nu, 2):
                 b = tpp.tile([P, 2, 2, P], F32, name="tp", tag="tp")
-                for a in range(2):
-                    v = 2 * j + a
+                for v in range(v0, min(v0 + 2, nu)):
                     for u in range(2):
                         if v >= nre[q]:
                             src = words[:, v * W + u:(v + 1) * W:2]
                         else:
-                            src = xr[q][:, v, u, :]
-                        nc.tensor.transpose(b[:, a, u, :], src, ident[:])
+                            src = xr[q][:, u, v, :]
+                        nc.tensor.transpose(b[:, v - v0, u, :], src, ident[:])
                 banks.append(b)
             tps[q] = banks
 
@@ -139,10 +142,11 @@ def tile_testmmrsmodel_t_kernel(tc, hidden_states, gate_proj, world_size, out_0,
             nu = len(units(q))
             g = work.tile([P, nu * 4 * P], BF16, name="gq", tag="gq", align_bytes=64)
             gw = g[:].bitcast(F32).rearrange("p (v r u) -> p v r u", v=nu, u=2)
-            for j in range(nu // 2):
+            for j, v0 in enumerate(range(0, nu, 2)):
+                k = min(2, nu - v0)
                 nc.scalar.copy(
-                    out=gw[:, 2 * j:2 * j + 2, :, :],
-                    in_=tps[q][j][:].rearrange("p v u r -> p v r u"),
+                    out=gw[:, v0:v0 + k, :, :],
+                    in_=tps[q][j][:, 0:k, :, :].rearrange("p v u r -> p v r u"),
                 )
             gqs[q] = g
 
@@ -167,41 +171,54 @@ def tile_testmmrsmodel_t_kernel(tc, hidden_states, gate_proj, world_size, out_0,
                     stop=(r == R - 1),
                 )
                 if r == R - 1:
-                    closed.append((ib, l))
-            for ib, l in closed:
-                i = ib * NL + l
-                nc.scalar.copy(out=out_sb[:, i * O:(i + 1) * O], in_=acc[l][:, ib, :])
+                    closed.append(ib * NL + l)
+            for i in closed:
+                if i < (NB - 1) * NL:
+                    nc.vector.tensor_copy(out=out_sb[:, i * O:(i + 1) * O], in_=acc[i % NL][:, i // NL, :])
+                else:
+                    nc.scalar.copy(out=out_sb[:, i * O:(i + 1) * O], in_=acc[i % NL][:, i // NL, :])
             return closed
 
-        def finish_block(ib):
-            cols = slice(ib * NL * O, (ib + 1) * NL * O)
-            nc.vector.tensor_reduce(
-                out=pm[:, ib:ib + 1], in_=out_sb[:, cols], axis=AX.X, op=ALU.max,
-                apply_absolute_value=True,
-            )
-            nc.sync.dma_start(out=o0[:, cols], in_=out_sb[:, cols])
+        nparts = [0]
+
+        def finish(closed):
+            lo = closed[0] * O
+            hi = (closed[-1] + 1) * O
+            if closed[-1] == I - 1:
+                nc.vector.tensor_reduce(
+                    out=pmx[:], in_=out_sb[:, lo:hi + nparts[0]], axis=AX.X, op=ALU.max,
+                    apply_absolute_value=True,
+                )
+            else:
+                k = I * O + nparts[0]
+                nc.vector.tensor_reduce(
+                    out=out_sb[:, k:k + 1], in_=out_sb[:, lo:hi], axis=AX.X, op=ALU.max,
+                    apply_absolute_value=True,
+                )
+                nparts[0] = nparts[0] + 1
+            nc.sync.dma_start(out=o0[:, lo:hi], in_=out_sb[:, lo:hi])
 
         pending = []
         for s in range(-1, n + 3):
-            if 0 <= s - 2 < n:
-                quantize(s - 2)
-            for ib in pending:
-                finish_block(ib)
-            pending = []
-            if s + 1 < n:
-                reorder(s + 1)
             if 0 <= s - 1 < n:
                 transpose(s - 1)
                 evacuate(s - 1)
+            if s == 2:
+                prepare_gate()
+            if 0 <= s - 2 < n:
+                quantize(s - 2)
+            for closed in pending:
+                finish(closed)
+            pending = []
+            if s + 1 < n:
+                reorder(s + 1)
             if 0 <= s - 3 < n:
                 closed = multiply(s - 3)
-                if (closed and closed[-1][1] == NL - 1):
-                    pending.append(closed[-1][0])
-        for ib in pending:
-            finish_block(ib)
+                if closed:
+                    pending.append(closed)
+        for closed in pending:
+            finish(closed)
 
-        pmx = const.tile([P, 1], F32, name="pmx")
-        nc.vector.tensor_reduce(out=pmx[:], in_=pm[:], axis=AX.X, op=ALU.max)
         bc = tpp.tile([P, P], F32, name="tp", tag="tp")
         nc.tensor.transpose(bc[:], pmx[:, 0:1].to_broadcast([P, P]), ident[:])
         junk = const.tile([P, P], F32, name="junk")
@@ -218,7 +235,7 @@ def tile_testmmrsmodel_t_kernel(tc, hidden_states, gate_proj, world_size, out_0,
             op0=ALU.mult, saturate=False,
         )
         nc.scalar.activation(
-            out=o8[:, V_CAST:], in_=out_sb[:, V_CAST:], func=ACT.Identity,
+            out=o8[:, V_CAST:], in_=out_sb[:, V_CAST:I * O], func=ACT.Identity,
             scale=fac[:, 0:1], bias=zero[:, 0:1], saturate=False,
         )
         nc.sync.dma_start(out=o1, in_=o8[:].bitcast(U8))

@@ -50,13 +50,14 @@ def tile_testmmrsmodel_t_kernel(tc, hidden_states, gate_proj, world_size, out_0,
     nre = []
     for q in range(n):
         nu = pieces[q][2] * pieces[q][4]
-        nre.append(0 if (q < 2 or q >= n - 3) else nu - (3 * nu) // 8)
+        nre.append(0 if (q < 2 or q >= n - 3) else nu - nu // 4)
 
     with ExitStack() as ctx:
         ctx.enter_context(tc.manual_schedule())
         const = ctx.enter_context(tc.tile_pool(name="const", bufs=1))
         rawp = ctx.enter_context(tc.tile_pool(name="rawp", bufs=1))
         work = ctx.enter_context(tc.tile_pool(name="work", bufs=3))
+        codes = ctx.enter_context(tc.tile_pool(name="codes", bufs=5))
         tpp = ctx.enter_context(tc.psum_pool(name="tpp", bufs=4))
         accp = ctx.enter_context(tc.psum_pool(name="accp", bufs=1))
 
@@ -140,7 +141,10 @@ def tile_testmmrsmodel_t_kernel(tc, hidden_states, gate_proj, world_size, out_0,
 
         def evacuate(q):
             nu = len(units(q))
-            g = work.tile([P, nu * 4 * P], BF16, name="gq", tag="gq", align_bytes=64)
+            if q >= n - 4:
+                g = const.tile([P, nu * 4 * P], BF16, name="gq_last%d" % q, align_bytes=64)
+            else:
+                g = work.tile([P, nu * 4 * P], BF16, name="gq", tag="gq", align_bytes=64)
             gw = g[:].bitcast(F32).rearrange("p (v r u) -> p v r u", v=nu, u=2)
             for j, v0 in enumerate(range(0, nu, 2)):
                 k = min(2, nu - v0)
@@ -152,8 +156,8 @@ def tile_testmmrsmodel_t_kernel(tc, hidden_states, gate_proj, world_size, out_0,
 
         def quantize(q):
             nu = len(units(q))
-            c = work.tile([P, nu * P], U32, name="cd", tag="cd", align_bytes=64)
-            s = work.tile([P, nu * P], U8, name="sc", tag="sc", align_bytes=64)
+            c = codes.tile([P, nu * P], U32, name="cd", tag="cd", align_bytes=64)
+            s = codes.tile([P, nu * P], U8, name="sc", tag="sc", align_bytes=64)
             nc.vector.quantize_mx(out=c[:].bitcast(FP8X4), scales=s[:], in_=gqs[q][:])
             cds[q] = c
             scs[q] = s
@@ -198,11 +202,17 @@ def tile_testmmrsmodel_t_kernel(tc, hidden_states, gate_proj, world_size, out_0,
                 nparts[0] = nparts[0] + 1
             nc.sync.dma_start(out=o0[:, lo:hi], in_=out_sb[:, lo:hi])
 
+        held = [False] * n
+        first_small = n - 4
         pending = []
         for s in range(-1, n + 3):
-            if 0 <= s - 1 < n:
+            if 0 <= s - 1 < first_small:
                 transpose(s - 1)
                 evacuate(s - 1)
+            elif s - 1 == first_small:
+                for q in range(first_small, n):
+                    transpose(q)
+                    evacuate(q)
             if s == 2:
                 prepare_gate()
             if 0 <= s - 2 < n:
@@ -210,12 +220,14 @@ def tile_testmmrsmodel_t_kernel(tc, hidden_states, gate_proj, world_size, out_0,
             for closed in pending:
                 finish(closed)
             pending = []
-            if s + 1 < n:
-                reorder(s + 1)
-            if 0 <= s - 3 < n:
+            if 0 <= s - 3 < n and not held[s - 3]:
+                if s - 4 >= 0 and held[s - 4]:
+                    multiply(s - 4)
                 closed = multiply(s - 3)
                 if closed:
                     pending.append(closed)
+            if s + 1 < n:
+                reorder(s + 1)
         for closed in pending:
             finish(closed)
 

@@ -27,6 +27,7 @@ FLOPS = 2 * R * S * H * O
 
 V_CAST = 1344
 NPART = 8
+V_EVERY = 99
 
 
 def tile_testmmrsmodel_t_kernel(tc, hidden_states, gate_proj, world_size, out_0, out_1):
@@ -43,14 +44,14 @@ def tile_testmmrsmodel_t_kernel(tc, hidden_states, gate_proj, world_size, out_0,
             if ib == 0 and r0 == 0:
                 pieces.extend([(ib, 0, 1, 0, 2), (ib, 0, 1, 2, 2), (ib, 1, 1, 0, 4)])
             elif ib == NB - 1 and r0 == R - 2:
-                pieces.extend([(ib, r0, 1, 0, 4), (ib, r0 + 1, 1, 0, 2), (ib, r0 + 1, 1, 2, 1), (ib, r0 + 1, 1, 3, 1)])
+                pieces.extend([(ib, r0, 1, 0, 4), (ib, r0 + 1, 1, 0, 2), (ib, r0 + 1, 1, 2, 2)])
             else:
                 pieces.append((ib, r0, 2, 0, 4))
     n = len(pieces)
     nre = []
     for q in range(n):
         nu = pieces[q][2] * pieces[q][4]
-        nre.append(0 if (q < 2 or q >= n - 3) else nu - nu // 4)
+        nre.append(0 if (q < 2 or q >= n - 2) else (nu // 2 if q % 2 == 0 else nu - nu // 4))
 
     with ExitStack() as ctx:
         ctx.enter_context(tc.manual_schedule())
@@ -116,10 +117,10 @@ def tile_testmmrsmodel_t_kernel(tc, hidden_states, gate_proj, world_size, out_0,
             nu = len(units(q))
             if nre[q] == 0:
                 return
-            t = work.tile([P, 2, nre[q], P], F32, name="xr", tag="xr")
+            t = work.tile([P, nre[q], 2, P], F32, name="xr", tag="xr")
             nc.vector.tensor_copy(
                 out=t[:],
-                in_=raw[q][:].bitcast(F32).rearrange("p (v w u) -> p u v w", v=nu, u=2)[:, :, 0:nre[q], :],
+                in_=raw[q][:].bitcast(F32).rearrange("p (v w u) -> p v u w", v=nu, u=2)[:, 0:nre[q], :, :],
             )
             xr[q] = t
 
@@ -134,24 +135,30 @@ def tile_testmmrsmodel_t_kernel(tc, hidden_states, gate_proj, world_size, out_0,
                         if v >= nre[q]:
                             src = words[:, v * W + u:(v + 1) * W:2]
                         else:
-                            src = xr[q][:, u, v, :]
+                            src = xr[q][:, v, u, :]
                         nc.tensor.transpose(b[:, v - v0, u, :], src, ident[:])
                 banks.append(b)
             tps[q] = banks
 
         def evacuate(q):
             nu = len(units(q))
-            if q >= n - 4:
+            if q >= n - 3:
                 g = const.tile([P, nu * 4 * P], BF16, name="gq_last%d" % q, align_bytes=64)
             else:
                 g = work.tile([P, nu * 4 * P], BF16, name="gq", tag="gq", align_bytes=64)
             gw = g[:].bitcast(F32).rearrange("p (v r u) -> p v r u", v=nu, u=2)
             for j, v0 in enumerate(range(0, nu, 2)):
                 k = min(2, nu - v0)
-                nc.scalar.copy(
-                    out=gw[:, v0:v0 + k, :, :],
-                    in_=tps[q][j][:, 0:k, :, :].rearrange("p v u r -> p v r u"),
-                )
+                if j == 0 and nu == 8 and q % V_EVERY == 0:
+                    nc.vector.tensor_copy(
+                        out=gw[:, v0:v0 + k, :, :],
+                        in_=tps[q][j][:, 0:k, :, :].rearrange("p v u r -> p v r u"),
+                    )
+                else:
+                    nc.scalar.copy(
+                        out=gw[:, v0:v0 + k, :, :],
+                        in_=tps[q][j][:, 0:k, :, :].rearrange("p v u r -> p v r u"),
+                    )
             gqs[q] = g
 
         def quantize(q):
@@ -200,10 +207,14 @@ def tile_testmmrsmodel_t_kernel(tc, hidden_states, gate_proj, world_size, out_0,
                     apply_absolute_value=True,
                 )
                 nparts[0] = nparts[0] + 1
-            nc.sync.dma_start(out=o0[:, lo:hi], in_=out_sb[:, lo:hi])
+            if closed[-1] < (NB - 1) * NL:
+                nc.sync.dma_start(out=o0[:, lo:hi], in_=out_sb[:, lo:hi])
+            elif closed[-1] == I - 1:
+                lo = (NB - 1) * NL * O
+                nc.scalar.dma_start(out=o0[:, lo:hi], in_=out_sb[:, lo:hi])
 
         held = [False] * n
-        first_small = n - 4
+        first_small = n - 3
         pending = []
         for s in range(-1, n + 3):
             if 0 <= s - 1 < first_small:

@@ -27,7 +27,6 @@ FLOPS = 2 * R * S * H * O
 
 V_CAST = 1344
 NPART = 8
-V_EVERY = 99
 
 
 def tile_testmmrsmodel_t_kernel(tc, hidden_states, gate_proj, world_size, out_0, out_1):
@@ -128,15 +127,17 @@ def tile_testmmrsmodel_t_kernel(tc, hidden_states, gate_proj, world_size, out_0,
             nu = len(units(q))
             words = raw[q][:].bitcast(F32)
             banks = []
-            for v0 in range(0, nu, 2):
+            nb = nu // 2
+            for j in range(nb):
                 b = tpp.tile([P, 2, 2, P], F32, name="tp", tag="tp")
-                for v in range(v0, min(v0 + 2, nu)):
+                for e in range(2):
+                    v = j + e * nb
                     for u in range(2):
                         if v >= nre[q]:
                             src = words[:, v * W + u:(v + 1) * W:2]
                         else:
                             src = xr[q][:, v, u, :]
-                        nc.tensor.transpose(b[:, v - v0, u, :], src, ident[:])
+                        nc.tensor.transpose(b[:, e, u, :], src, ident[:])
                 banks.append(b)
             tps[q] = banks
 
@@ -147,18 +148,12 @@ def tile_testmmrsmodel_t_kernel(tc, hidden_states, gate_proj, world_size, out_0,
             else:
                 g = work.tile([P, nu * 4 * P], BF16, name="gq", tag="gq", align_bytes=64)
             gw = g[:].bitcast(F32).rearrange("p (v r u) -> p v r u", v=nu, u=2)
-            for j, v0 in enumerate(range(0, nu, 2)):
-                k = min(2, nu - v0)
-                if j == 0 and nu == 8 and q % V_EVERY == 0:
-                    nc.vector.tensor_copy(
-                        out=gw[:, v0:v0 + k, :, :],
-                        in_=tps[q][j][:, 0:k, :, :].rearrange("p v u r -> p v r u"),
-                    )
-                else:
-                    nc.scalar.copy(
-                        out=gw[:, v0:v0 + k, :, :],
-                        in_=tps[q][j][:, 0:k, :, :].rearrange("p v u r -> p v r u"),
-                    )
+            nb = nu // 2
+            for j in range(nb):
+                nc.scalar.copy(
+                    out=gw[:, j:nu:nb, :, :],
+                    in_=tps[q][j][:].rearrange("p v u r -> p v r u"),
+                )
             gqs[q] = g
 
         def quantize(q):

@@ -248,12 +248,15 @@ def tile_testmmrsmodel_t_kernel(tc, hidden_states, gate_proj, world_size, out_0,
         fac = const.tile([P, 1], F32, name="fac")
         nc.vector.reciprocal(out=fac[:], in_=sc448[:])
         o8 = const.tile([P, I * O], FP8, name="o8")
-        nc.vector.tensor_scalar(
-            out=o8[:, 0:V_CAST], in0=out_sb[:, 0:V_CAST], scalar1=fac[:, 0:1], scalar2=None,
-            op0=ALU.mult, saturate=False,
-        )
-        nc.scalar.activation(
-            out=o8[:, V_CAST:], in_=out_sb[:, V_CAST:I * O], func=ACT.Identity,
-            scale=fac[:, 0:1], bias=zero[:, 0:1], saturate=False,
-        )
-        nc.sync.dma_start(out=o1, in_=o8[:].bitcast(U8))
+        for lo, hi in ((0, 832), (832, 1344)):
+            nc.vector.tensor_scalar(
+                out=o8[:, lo:hi], in0=out_sb[:, lo:hi], scalar1=fac[:, 0:1], scalar2=None,
+                op0=ALU.mult, saturate=False,
+            )
+        for lo, hi in ((1344, 1792), (1792, I * O)):
+            nc.scalar.activation(
+                out=o8[:, lo:hi], in_=out_sb[:, lo:hi], func=ACT.Identity,
+                scale=fac[:, 0:1], bias=zero[:, 0:1], saturate=False,
+            )
+        for lo, hi in ((0, 832), (1344, 1792), (832, 1344), (1792, I * O)):
+            nc.sync.dma_start(out=o1[:, lo:hi], in_=o8[:, lo:hi].bitcast(U8))

@@ -72,10 +72,11 @@ def tile_testmmrsmodel_t_kernel(tc, hidden_states, gate_proj, world_size, out_0,
             ib, r0, nr, l0, nl = pieces[q]
             t = rawp.tile([P, nr * nl * H], BF16, name="raw%d" % q)
             i0 = ib * NL + l0
-            nc.sync.dma_start(
-                out=t[:].rearrange("p (a x) -> p a x", a=nr),
-                in_=hs[:, r0:r0 + nr, i0 * H:(i0 + nl) * H],
-            )
+            for a in range(nr):
+                nc.sync.dma_start(
+                    out=t[:, a * nl * H:(a + 1) * nl * H],
+                    in_=hs[:, r0 + a, i0 * H:(i0 + nl) * H],
+                )
             raw.append(t)
             if q == 1:
                 nc.sync.dma_start(out=g_raw[:], in_=gate_proj)
@@ -117,10 +118,12 @@ def tile_testmmrsmodel_t_kernel(tc, hidden_states, gate_proj, world_size, out_0,
             if nre[q] == 0:
                 return
             t = work.tile([P, nre[q], 2, P], F32, name="xr", tag="xr")
-            nc.vector.tensor_copy(
-                out=t[:],
-                in_=raw[q][:].bitcast(F32).rearrange("p (v w u) -> p v u w", v=nu, u=2)[:, 0:nre[q], :, :],
-            )
+            for v0 in range(0, nre[q], 4):
+                v1 = min(v0 + 4, nre[q])
+                nc.vector.tensor_copy(
+                    out=t[:, v0:v1, :, :],
+                    in_=raw[q][:].bitcast(F32).rearrange("p (v w u) -> p v u w", v=nu, u=2)[:, v0:v1, :, :],
+                )
             xr[q] = t
 
         def transpose(q):
@@ -211,6 +214,7 @@ def tile_testmmrsmodel_t_kernel(tc, hidden_states, gate_proj, world_size, out_0,
         held = [False] * n
         first_small = n - 3
         pending = []
+        late = []
         for s in range(-1, n + 3):
             if 0 <= s - 1 < first_small:
                 transpose(s - 1)
@@ -224,8 +228,14 @@ def tile_testmmrsmodel_t_kernel(tc, hidden_states, gate_proj, world_size, out_0,
             if 0 <= s - 2 < n:
                 quantize(s - 2)
             for closed in pending:
-                finish(closed)
+                if closed[-1] == (NB - 1) * NL - 1:
+                    late.append(closed)
+                else:
+                    finish(closed)
             pending = []
+            if s - 2 == n - 1:
+                for closed in late:
+                    finish(closed)
             if 0 <= s - 3 < n and not held[s - 3]:
                 if s - 4 >= 0 and held[s - 4]:
                     multiply(s - 4)

from contextlib import ExitStack

import concourse.masks as masks
import concourse.mybir as mybir

F32 = mybir.dt.float32
BF16 = mybir.dt.bfloat16
U32 = mybir.dt.uint32
U8 = mybir.dt.uint8
FP8X4 = mybir.dt.float8_e4m3fn_x4
FP8 = mybir.dt.float8_e4m3fn
ALU = mybir.AluOpType
ACT = mybir.ActivationFunctionType
AX = mybir.AxisListType

P = 128
R = 8
S = 2048
H = 512
O = 128
I = S // P
NL = 4
NB = I // NL
W = H // 2

FLOPS = 2 * R * S * H * O

V_CAST = 1344
NPART = 8


def tile_testmmrsmodel_t_kernel(tc, hidden_states, gate_proj, world_size, out_0, out_1):
    nc = tc.nc
    assert world_size == R

    hs = hidden_states.rearrange("r (p i) k -> p r (i k)", i=I)
    o0 = out_0.rearrange("(p i) o -> p (i o)", i=I)
    o1 = out_1.rearrange("(p i) o -> p (i o)", i=I)

    pieces = []
    for ib in range(NB):
        for r0 in range(0, R, 2):
            if ib == 0 and r0 == 0:
                pieces.extend([(ib, 0, 1, 0, 2), (ib, 0, 1, 2, 2), (ib, 1, 1, 0, 4)])
            elif ib == NB - 1 and r0 == R - 2:
                pieces.extend([(ib, r0, 1, 0, 4), (ib, r0 + 1, 1, 0, 2), (ib, r0 + 1, 1, 2, 2)])
            else:
                pieces.append((ib, r0, 2, 0, 4))
    n = len(pieces)
    nre = []
    for q in range(n):
        nu = pieces[q][2] * pieces[q][4]
        nre.append(0 if (q < 2 or q >= n - 2) else (nu // 2 if q % 2 == 0 else nu - nu // 4))

    with ExitStack() as ctx:
        ctx.enter_context(tc.manual_schedule())
        const = ctx.enter_context(tc.tile_pool(name="const", bufs=1))
        rawp = ctx.enter_context(tc.tile_pool(name="rawp", bufs=1))
        work = ctx.enter_context(tc.tile_pool(name="work", bufs=3))
        codes = ctx.enter_context(tc.tile_pool(name="codes", bufs=5))
        tpp = ctx.enter_context(tc.psum_pool(name="tpp", bufs=4))
        accp = ctx.enter_context(tc.psum_pool(name="accp", bufs=1))

        ident = const.tile([P, P], F32, name="ident")
        masks.make_identity(nc, ident[:])
        zero = const.tile([P, 1], F32, name="zero")
        nc.vector.memset(zero[:], 0.0)

        g_raw = const.tile([P, H], BF16, name="g_raw")
        raw = []
        for q in range(n):
            ib, r0, nr, l0, nl = pieces[q]
            t = rawp.tile([P, nr * nl * H], BF16, name="raw%d" % q)
            i0 = ib * NL + l0
            for a in range(nr):
                nc.sync.dma_start(
                    out=t[:, a * nl * H:(a + 1) * nl * H],
                    in_=hs[:, r0 + a, i0 * H:(i0 + nl) * H],
                )
            raw.append(t)
            if q == 1:
                nc.sync.dma_start(out=g_raw[:], in_=gate_proj)

        g_codes = const.tile([P, O], U32, name="g_codes", align_bytes=64)
        g_scales = const.tile([P, O], U8, name="g_scales", align_bytes=64)

        def prepare_gate():
            g_words = g_raw[:].bitcast(F32)
            g_tp = tpp.tile([P, 2, 2, P], F32, name="tp", tag="tp")
            for u in range(2):
                nc.tensor.transpose(g_tp[:, 0, u, :], g_words[:, u:W:2], ident[:])
            g_gq = const.tile([P, 4 * O], BF16, name="g_gq", align_bytes=64)
            nc.scalar.copy(
                out=g_gq[:].bitcast(F32).rearrange("p (r u) -> p r u", u=2),
                in_=g_tp[:, 0, :, :].rearrange("p u r -> p r u"),
            )
            nc.vector.quantize_mx(out=g_codes[:].bitcast(FP8X4), scales=g_scales[:], in_=g_gq[:])

        acc = []
        for l in range(NL):
            a = accp.tile([P, NB, O], F32, name="acc%d" % l)
            acc.append(a)
        out_sb = const.tile([P, I * O + NPART], F32, name="out_sb")
        pmx = const.tile([P, 1], F32, name="pmx")

        xr = [None] * n
        tps = [None] * n
        gqs = [None] * n
        cds = [None] * n
        scs = [None] * n

        def units(q):
            ib, r0, nr, l0, nl = pieces[q]
            return [(ib, l0 + b, r0 + a) for a in range(nr) for b in range(nl)]

        def reorder(q):
            nu = len(units(q))
            if nre[q] == 0:
                return
            t = work.tile([P, nre[q], 2, P], F32, name="xr", tag="xr")
            for v0 in range(0, nre[q], 4):
                v1 = min(v0 + 4, nre[q])
                nc.vector.tensor_copy(
                    out=t[:, v0:v1, :, :],
                    in_=raw[q][:].bitcast(F32).rearrange("p (v w u) -> p v u w", v=nu, u=2)[:, v0:v1, :, :],
                )
            xr[q] = t

        def transpose(q):
            nu = len(units(q))
            words = raw[q][:].bitcast(F32)
            banks = []
            nb = nu // 2
            for j in range(nb):
                b = tpp.tile([P, 2, 2, P], F32, name="tp", tag="tp")
                for e in range(2):
                    v = j + e * nb
                    for u in range(2):
                        if v >= nre[q]:
                            src = words[:, v * W + u:(v + 1) * W:2]
                        else:
                            src = xr[q][:, v, u, :]
                        nc.tensor.transpose(b[:, e, u, :], src, ident[:])
                banks.append(b)
            tps[q] = banks

        def evacuate(q):
            nu = len(units(q))
            if q >= n - 3:
                g = const.tile([P, nu * 4 * P], BF16, name="gq_last%d" % q, align_bytes=64)
            else:
                g = work.tile([P, nu * 4 * P], BF16, name="gq", tag="gq", align_bytes=64)
            gw = g[:].bitcast(F32).rearrange("p (v r u) -> p v r u", v=nu, u=2)
            nb = nu // 2
            for j in range(nb):
                nc.scalar.copy(
                    out=gw[:, j:nu:nb, :, :],
                    in_=tps[q][j][:].rearrange("p v u r -> p v r u"),
                )
            gqs[q] = g

        def quantize(q):
            nu = len(units(q))
            c = codes.tile([P, nu * P], U32, name="cd", tag="cd", align_bytes=64)
            s = codes.tile([P, nu * P], U8, name="sc", tag="sc", align_bytes=64)
            nc.vector.quantize_mx(out=c[:].bitcast(FP8X4), scales=s[:], in_=gqs[q][:])
            cds[q] = c
            scs[q] = s

        def multiply(q):
            closed = []
            for v, (ib, l, r) in enumerate(units(q)):
                nc.tensor.matmul_mx(
                    out=acc[l][:, ib, :],
                    lhsT=cds[q][:, v * P:(v + 1) * P].bitcast(FP8X4),
                    lhsT_scale=scs[q][:, v * P:(v + 1) * P],
                    rhs=g_codes[:].bitcast(FP8X4),
                    rhs_scale=g_scales[:],
                    start=(r == 0),
                    stop=(r == R - 1),
                )
                if r == R - 1:
                    closed.append(ib * NL + l)
            for i in closed:
                if i < (NB - 1) * NL:
                    nc.vector.tensor_copy(out=out_sb[:, i * O:(i + 1) * O], in_=acc[i % NL][:, i // NL, :])
                else:
                    nc.scalar.copy(out=out_sb[:, i * O:(i + 1) * O], in_=acc[i % NL][:, i // NL, :])
            return closed

        nparts = [0]

        def finish(closed):
            lo = closed[0] * O
            hi = (closed[-1] + 1) * O
            if closed[-1] == I - 1:
                nc.vector.tensor_reduce(
                    out=pmx[:], in_=out_sb[:, lo:hi + nparts[0]], axis=AX.X, op=ALU.max,
                    apply_absolute_value=True,
                )
            else:
                k = I * O + nparts[0]
                nc.vector.tensor_reduce(
                    out=out_sb[:, k:k + 1], in_=out_sb[:, lo:hi], axis=AX.X, op=ALU.max,
                    apply_absolute_value=True,
                )
                nparts[0] = nparts[0] + 1
            if closed[-1] < (NB - 1) * NL:
                nc.sync.dma_start(out=o0[:, lo:hi], in_=out_sb[:, lo:hi])
            elif closed[-1] == I - 1:
                lo = (NB - 1) * NL * O
                nc.scalar.dma_start(out=o0[:, lo:hi], in_=out_sb[:, lo:hi])

        held = [False] * n
        first_small = n - 3
        pending = []
        late = []
        for s in range(-1, n + 3):
            if 0 <= s - 1 < first_small:
                transpose(s - 1)
                evacuate(s - 1)
            elif s - 1 == first_small:
                for q in range(first_small, n):
                    transpose(q)
                    evacuate(q)
            if s == 2:
                prepare_gate()
            if 0 <= s - 2 < n:
                quantize(s - 2)
            for closed in pending:
                if closed[-1] == (NB - 1) * NL - 1:
                    late.append(closed)
                else:
                    finish(closed)
            pending = []
            if s - 2 == n - 1:
                for closed in late:
                    finish(closed)
            if 0 <= s - 3 < n and not held[s - 3]:
                if s - 4 >= 0 and held[s - 4]:
                    multiply(s - 4)
                closed = multiply(s - 3)
                if closed:
                    pending.append(closed)
            if s + 1 < n:
                reorder(s + 1)
        for closed in pending:
            finish(closed)

        bc = tpp.tile([P, P], F32, name="tp", tag="tp")
        nc.tensor.transpose(bc[:], pmx[:, 0:1].to_broadcast([P, P]), ident[:])
        junk = const.tile([P, P], F32, name="junk")
        sc448 = const.tile([P, 1], F32, name="sc448")
        nc.vector.tensor_scalar(
            out=junk[:], in0=bc[:], scalar1=1.0 / 448.0, scalar2=None,
            op0=ALU.mult, op1=ALU.max, accum_out=sc448[:, 0:1],
        )
        fac = const.tile([P, 1], F32, name="fac")
        nc.vector.reciprocal(out=fac[:], in_=sc448[:])
        o8 = const.tile([P, I * O], FP8, name="o8")
        for lo, hi in ((0, 832), (832, 1344)):
            nc.vector.tensor_scalar(
                out=o8[:, lo:hi], in0=out_sb[:, lo:hi], scalar1=fac[:, 0:1], scalar2=None,
                op0=ALU.mult, saturate=False,
            )
        for lo, hi in ((1344, 1792), (1792, I * O)):
            nc.scalar.activation(
                out=o8[:, lo:hi], in_=out_sb[:, lo:hi], func=ACT.Identity,
                scale=fac[:, 0:1], bias=zero[:, 0:1], saturate=False,
            )
        for lo, hi in ((0, 832), (1344, 1792), (832, 1344), (1792, I * O)):
            nc.sync.dma_start(out=o1[:, lo:hi], in_=o8[:, lo:hi].bitcast(U8))
